import numpy as np
import ml_dtypes


def mxq(x, axis, fmt="e4m3"):
    dtype, down = {"e4m3": (ml_dtypes.float8_e4m3fn, 7), "e5m2": (ml_dtypes.float8_e5m2, 14)}[fmt]
    v = np.moveaxis(np.asarray(x, np.float32).astype(ml_dtypes.bfloat16).astype(np.float64), axis, -1)
    blocks = v.reshape(v.shape[:-1] + (-1, 32))
    amax = np.abs(blocks).max(-1, keepdims=True)
    byte = np.maximum(np.where(amax > 0, np.frexp(amax)[1] - 1 + 127, 0) - down, 1)
    scale = np.exp2(byte - 127.0)
    codes = (blocks / scale).astype(np.float32).astype(dtype).astype(np.float64)
    return np.moveaxis((codes * scale).reshape(v.shape), -1, axis)


WIDE = False


def mx_kscale(k):
    if not WIDE:
        return np.ones(k)
    levels = np.array([20, -20, 10, -10, 0])
    a = np.random.permutation(np.resize(levels, k // 512 * 4)).reshape(k // 512, 4)
    idx = np.arange(k)
    return np.exp2(a[idx // 512, idx % 128 // 32])


BF16 = ml_dtypes.bfloat16


def bf(x):
    return np.asarray(x, np.float32).astype(BF16)


def f64(x):
    return np.asarray(x).astype(np.float64)


B, T, S, H, C, CO, W = 2, 128, 2, 8, 1024, 8192, 5
HD = C // H


def setup_inputs():
    u = mx_kscale(CO)
    i = np.arange(T)
    band = np.abs(i[:, None] - i[None, :]) <= W
    e = np.exp(np.random.standard_normal((B, H, S, T, T))) * band
    attn = e / e.sum(-1, keepdims=True)
    v = np.random.standard_normal((B, T, S, H, HD))
    w = np.random.standard_normal((C, CO)) / np.sqrt(C) / u[None, :]
    g = np.random.standard_normal((B, T * S, CO)) * np.exp2(np.random.randint(-12, 1, (B, T * S, 1))) * 16.0 * u
    return {"attn": bf(attn), "v": bf(v), "W_out": bf(w), "grad_out": bf(g)}


def reference(attn, v, W_out, grad_out):
    g = f64(grad_out).reshape(B * T * S, CO)
    gctx = mxq(g, 1, "e5m2") @ mxq(f64(W_out), 1, "e4m3").T
    gctx = gctx.reshape(B, T, S, H, HD).transpose(0, 3, 2, 1, 4)
    gv = f64(attn).transpose(0, 1, 2, 4, 3) @ gctx
    return np.ascontiguousarray(gv.transpose(0, 3, 2, 1, 4))

@@ -1,0 +1,204 @@
+from contextlib import ExitStack
+
+import concourse.mybir as mybir
+from concourse.masks import make_identity
+
+F32 = mybir.dt.float32
+BF16 = mybir.dt.bfloat16
+U32 = mybir.dt.uint32
+U8 = mybir.dt.uint8
+E5M2_X4 = mybir.dt.float8_e5m2_x4
+E4M3_X4 = mybir.dt.float8_e4m3fn_x4
+
+B, T, S, H, HD = 2, 128, 2, 8, 128
+C = H * HD
+CO = 8192
+
+P = 128
+PACK = 4
+K_PASS = P * PACK
+N_PASSES = CO // K_PASS
+ROW_TILES = 4
+PANEL_ROWS = ROW_TILES * P
+HALVES = C // PANEL_ROWS
+HEADS_PER_HALF = H // HALVES
+
+K_CHUNK = 2048
+PASSES_PER_CHUNK = K_CHUNK // K_PASS
+N_CHUNKS = CO // K_CHUNK
+RAW_BUFS = 6
+
+GRAD = 0
+LAST_HALF = HALVES
+
+FLOPS = 2 * B * T * S * C * CO + 2 * B * H * S * T * T * HD
+BYTES = 2 * (B * H * S * T * T + C * CO + B * T * S * CO) + 4 * B * T * S * C
+
+
+def tile_localtemporalattention_pa_k_kernel(tc, attn, v, W_out, grad_out, out):
+    nc = tc.nc
+
+    grad_rows = grad_out.rearrange("b (t s) k -> b t s k", s=S)
+    w_rows = W_out.rearrange("(half r p) k -> half p r k", half=HALVES, r=ROW_TILES)
+
+    chunk_order = []
+    for chunk in range(N_CHUNKS):
+        chunk_order.extend([(GRAD, chunk), (1, chunk)])
+    for chunk in range(N_CHUNKS):
+        chunk_order.append((LAST_HALF, chunk))
+
+    with ExitStack() as stack:
+        const = stack.enter_context(tc.tile_pool(name="const", bufs=1))
+        raw_pool = stack.enter_context(tc.tile_pool(name="raw", bufs=RAW_BUFS))
+        grouped_pool = stack.enter_context(tc.tile_pool(name="grouped", bufs=4))
+        grad_mx = stack.enter_context(tc.tile_pool(name="grad_mx", bufs=1))
+        w_mx = stack.enter_context(tc.tile_pool(name="w_mx", bufs=4))
+        gctx_pool = stack.enter_context(tc.tile_pool(name="gctx", bufs=1))
+        result_pool = stack.enter_context(tc.tile_pool(name="result", bufs=4))
+        acc_psum = stack.enter_context(tc.psum_pool(name="acc", bufs=1))
+        work_psum = stack.enter_context(tc.psum_pool(name="work", bufs=4))
+        stack.enter_context(tc.manual_schedule())
+
+        raw_of = {}
+        grouped_of = {}
+        codes_of = {}
+        scales_of = {}
+        acc_of = {}
+        gctx_of = {}
+
+        ident = const.tile([P, P], F32)
+        make_identity(nc, ident[:])
+
+        def new_raw(position):
+            raw_of[chunk_order[position]] = raw_pool.tile([P, ROW_TILES, K_CHUNK], BF16, tag="raw", name="raw")
+
+        def load_passes(position, first_pass, n_passes):
+            operand, chunk = chunk_order[position]
+            raw = raw_of[(operand, chunk)]
+            lo = first_pass * K_PASS
+            hi = lo + n_passes * K_PASS
+            k_lo = chunk * K_CHUNK + lo
+            k_hi = chunk * K_CHUNK + hi
+            if operand == GRAD:
+                for b in range(B):
+                    nc.sync.dma_start(out=raw[:, S * b : S * b + S, lo:hi], in_=grad_rows[b, :, :, k_lo:k_hi])
+            else:
+                nc.sync.dma_start(out=raw[:, :, lo:hi], in_=w_rows[operand - 1, :, :, k_lo:k_hi])
+
+        def load_chunk(position):
+            if position < len(chunk_order):
+                new_raw(position)
+                load_passes(position, 0, PASSES_PER_CHUNK)
+
+        def transpose_panel(operand, k_pass):
+            chunk, pass_in_chunk = divmod(k_pass, PASSES_PER_CHUNK)
+            words = raw_of[(operand, chunk)][:].bitcast(F32)
+            banks = []
+            for pair in range(ROW_TILES // 2):
+                bank = work_psum.tile([P, 2, 2 * P], F32, tag="bank", name="bank")
+                for r in range(2):
+                    for u in range(2):
+                        first_word = pass_in_chunk * (K_PASS // 2) + u * P
+                        nc.tensor.transpose(
+                            bank[:, u, r * P : (r + 1) * P],
+                            words[:, 2 * pair + r, first_word : first_word + P],
+                            ident[:],
+                        )
+                banks.append(bank)
+            if pass_in_chunk == PASSES_PER_CHUNK - 1:
+                load_chunk(chunk_order.index((operand, chunk)) + RAW_BUFS)
+            return banks
+
+        def regroup_panel(operand, k_pass, banks, copies):
+            grouped = grouped_pool.tile([P, PANEL_ROWS * PACK], BF16, tag="grouped", name="grouped", align_bytes=64)
+            halves = grouped[:].bitcast(F32).rearrange("p (pair n u) -> p pair n u", pair=2, u=2)
+            for pair in range(2):
+                copies[pair](out=halves[:, pair], in_=banks[pair][:].rearrange("p u n -> p n u"))
+            grouped_of[(operand, k_pass)] = grouped
+
+        def quantise_panel(operand, k_pass):
+            if operand == GRAD:
+                codes = grad_mx.tile([P, PANEL_ROWS], U32, name="grad_codes%d" % k_pass, align_bytes=64)
+                scales = grad_mx.tile([P, PANEL_ROWS], U8, name="grad_scales%d" % k_pass, align_bytes=64)
+                fp8_x4 = E5M2_X4
+            else:
+                codes = w_mx.tile([P, PANEL_ROWS], U32, tag="w_codes", name="w_codes", align_bytes=64)
+                scales = w_mx.tile([P, PANEL_ROWS], U8, tag="w_scales", name="w_scales", align_bytes=64)
+                fp8_x4 = E4M3_X4
+            nc.vector.quantize_mx(out=codes[:].bitcast(fp8_x4), scales=scales[:], in_=grouped_of[(operand, k_pass)][:])
+            codes_of[(operand, k_pass)] = codes
+            scales_of[(operand, k_pass)] = scales
+
+        def multiply_pass(half, k_pass):
+            for i in range(ROW_TILES):
+                if k_pass == 0:
+                    acc_of[(half, i)] = acc_psum.tile([P, PANEL_ROWS], F32, tag="acc%d" % i, name="acc%d" % i)
+                rows = slice(i * P, (i + 1) * P)
+                nc.tensor.matmul_mx(
+                    out=acc_of[(half, i)][:],
+                    lhsT=codes_of[(GRAD, k_pass)][:, rows].bitcast(E5M2_X4),
+                    lhsT_scale=scales_of[(GRAD, k_pass)][:, rows],
+                    rhs=codes_of[(1 + half, k_pass)][:].bitcast(E4M3_X4),
+                    rhs_scale=scales_of[(1 + half, k_pass)][:],
+                    start=(k_pass == 0),
+                    stop=(k_pass == N_PASSES - 1),
+                )
+
+        def alternate_copy(i):
+            return nc.scalar.copy if i % 2 == 0 else nc.vector.tensor_copy
+
+        def save_gctx(half):
+            for i in range(ROW_TILES):
+                gctx = gctx_pool.tile([P, PANEL_ROWS], F32, name="gctx%d_%d" % (half, i))
+                alternate_copy(i)(out=gctx[:], in_=acc_of[(half, i)][:])
+                gctx_of[(half, i)] = gctx
+
+        def pipeline_step(fresh, ready):
+            banks = [transpose_panel(operand, k_pass) for operand, k_pass in fresh]
+            for operand, k_pass in ready:
+                quantise_panel(operand, k_pass)
+            engine_copies = [(nc.scalar.copy, nc.scalar.copy), (nc.scalar.copy, nc.vector.tensor_copy)]
+            for (operand, k_pass), panel_banks, copies in zip(fresh, banks, engine_copies):
+                regroup_panel(operand, k_pass, panel_banks, copies)
+                if operand == LAST_HALF:
+                    matrices = slice(2 * k_pass, 2 * k_pass + 2)
+                    nc.scalar.copy(out=attn_f32[:, matrices, :], in_=attn_bf16[:, matrices, :])
+            for operand, k_pass in ready:
+                if operand != GRAD:
+                    multiply_pass(operand - 1, k_pass)
+                    if k_pass == N_PASSES - 1:
+                        save_gctx(operand - 1)
+
+        new_raw(0)
+        new_raw(1)
+        for k_pass in range(PASSES_PER_CHUNK):
+            load_passes(0, k_pass, 1)
+            load_passes(1, k_pass, 1)
+        for position in range(2, RAW_BUFS):
+            load_chunk(position)
+        attn_bf16 = const.tile([P, B * H * S, T], BF16)
+        attn_f32 = const.tile([P, B * H * S, T], F32)
+        nc.sync.dma_start(out=attn_bf16[:], in_=attn.rearrange("b h s t u -> t (b h s) u"))
+
+        steps = [[(GRAD, k_pass), (1, k_pass)] for k_pass in range(N_PASSES)]
+        steps.extend([[(LAST_HALF, k_pass), (LAST_HALF, k_pass + 1)] for k_pass in range(0, N_PASSES, 2)])
+        for fresh, ready in zip(steps + [[]], [[]] + steps):
+            pipeline_step(fresh, ready)
+
+        for half in range(HALVES):
+            for i in range(ROW_TILES):
+                b, s = divmod(i, S)
+                mixed = work_psum.tile([P, HEADS_PER_HALF, HD], F32, tag="bank", name="mixed")
+                for r in range(HEADS_PER_HALF):
+                    h = half * HEADS_PER_HALF + r
+                    nc.tensor.matmul(
+                        out=mixed[:, r, :],
+                        lhsT=attn_f32[:, (b * H + h) * S + s, :],
+                        rhs=gctx_of[(half, i)][:, r * HD : (r + 1) * HD],
+                        start=True,
+                        stop=True,
+                    )
+                result = result_pool.tile([P, HEADS_PER_HALF, HD], F32, tag="result", name="result")
+                alternate_copy(i)(out=result[:], in_=mixed[:])
+                first_head = half * HEADS_PER_HALF
+                nc.sync.dma_start(out=out[b, :, s, first_head : first_head + HEADS_PER_HALF, :], in_=result[:])

@@ -59,7 +59,8 @@ def tile_localtemporalattention_pa_k_kernel(tc, attn, v, W_out, grad_out, out):
         work_psum = stack.enter_context(tc.psum_pool(name="work", bufs=4))
         stack.enter_context(tc.manual_schedule())
 
-        raw_of = {}
+        panel_of = {}
+        words_of = {}
         grouped_of = {}
         codes_of = {}
         scales_of = {}
@@ -69,40 +70,40 @@ def tile_localtemporalattention_pa_k_kernel(tc, attn, v, W_out, grad_out, out):
         ident = const.tile([P, P], F32)
         make_identity(nc, ident[:])
 
-        def new_raw(position):
-            raw_of[chunk_order[position]] = raw_pool.tile([P, ROW_TILES, K_CHUNK], BF16, tag="raw", name="raw")
-
-        def load_passes(position, first_pass, n_passes):
-            operand, chunk = chunk_order[position]
-            raw = raw_of[(operand, chunk)]
-            lo = first_pass * K_PASS
-            hi = lo + n_passes * K_PASS
-            k_lo = chunk * K_CHUNK + lo
-            k_hi = chunk * K_CHUNK + hi
+        def load_features(operand, k_lo, k_hi, dst):
             if operand == GRAD:
                 for b in range(B):
-                    nc.sync.dma_start(out=raw[:, S * b : S * b + S, lo:hi], in_=grad_rows[b, :, :, k_lo:k_hi])
+                    nc.sync.dma_start(out=dst[:, S * b : S * b + S, :], in_=grad_rows[b, :, :, k_lo:k_hi])
             else:
-                nc.sync.dma_start(out=raw[:, :, lo:hi], in_=w_rows[operand - 1, :, :, k_lo:k_hi])
+                nc.sync.dma_start(out=dst, in_=w_rows[operand - 1, :, :, k_lo:k_hi])
+
+        def new_chunk(position, layout):
+            operand, chunk = chunk_order[position]
+            raw = raw_pool.tile([P, ROW_TILES * K_CHUNK], BF16, tag="raw", name="raw")
+            panels = raw[:].rearrange(layout + " -> p c r k", c=PASSES_PER_CHUNK, r=ROW_TILES)
+            words = raw[:].bitcast(F32).rearrange(layout + " -> p c r k", c=PASSES_PER_CHUNK, r=ROW_TILES)
+            for c in range(PASSES_PER_CHUNK):
+                panel_of[(operand, chunk * PASSES_PER_CHUNK + c)] = panels[:, c]
+                words_of[(operand, chunk * PASSES_PER_CHUNK + c)] = words[:, c]
+            return raw
 
         def load_chunk(position):
             if position < len(chunk_order):
-                new_raw(position)
-                load_passes(position, 0, PASSES_PER_CHUNK)
+                operand, chunk = chunk_order[position]
+                raw = new_chunk(position, "p (r c k)")
+                dst = raw[:].rearrange("p (r k) -> p r k", r=ROW_TILES)
+                load_features(operand, chunk * K_CHUNK, (chunk + 1) * K_CHUNK, dst)
 
         def transpose_panel(operand, k_pass):
             chunk, pass_in_chunk = divmod(k_pass, PASSES_PER_CHUNK)
-            words = raw_of[(operand, chunk)][:].bitcast(F32)
+            words = words_of[(operand, k_pass)]
             banks = []
             for pair in range(ROW_TILES // 2):
                 bank = work_psum.tile([P, 2, 2 * P], F32, tag="bank", name="bank")
                 for r in range(2):
                     for u in range(2):
-                        first_word = pass_in_chunk * (K_PASS // 2) + u * P
                         nc.tensor.transpose(
-                            bank[:, u, r * P : (r + 1) * P],
-                            words[:, 2 * pair + r, first_word : first_word + P],
-                            ident[:],
+                            bank[:, u, r * P : (r + 1) * P], words[:, 2 * pair + r, u * P : (u + 1) * P], ident[:]
                         )
                 banks.append(bank)
             if pass_in_chunk == PASSES_PER_CHUNK - 1:
@@ -169,11 +170,11 @@ def tile_localtemporalattention_pa_k_kernel(tc, attn, v, W_out, grad_out, out):
                     if k_pass == N_PASSES - 1:
                         save_gctx(operand - 1)
 
-        new_raw(0)
-        new_raw(1)
+        new_chunk(0, "p (c r k)")
+        new_chunk(1, "p (c r k)")
         for k_pass in range(PASSES_PER_CHUNK):
-            load_passes(0, k_pass, 1)
-            load_passes(1, k_pass, 1)
+            for operand in (GRAD, 1):
+                load_features(operand, k_pass * K_PASS, (k_pass + 1) * K_PASS, panel_of[(operand, k_pass)])
         for position in range(2, RAW_BUFS):
             load_chunk(position)
         attn_bf16 = const.tile([P, B * H * S, T], BF16)

@@ -23,13 +23,16 @@ PANEL_ROWS = ROW_TILES * P
 HALVES = C // PANEL_ROWS
 HEADS_PER_HALF = H // HALVES
 
-K_CHUNK = 2048
+K_CHUNK = 1024
 PASSES_PER_CHUNK = K_CHUNK // K_PASS
 N_CHUNKS = CO // K_CHUNK
-RAW_BUFS = 6
+RAW_BUFS = 12
 
 GRAD = 0
 LAST_HALF = HALVES
+ATTN_BEHIND = (LAST_HALF, 1)
+N_MATRICES = B * H * S
+CAST_PANELS = N_PASSES // 2
 
 FLOPS = 2 * B * T * S * C * CO + 2 * B * H * S * T * T * HD
 BYTES = 2 * (B * H * S * T * T + C * CO + B * T * S * CO) + 4 * B * T * S * C
@@ -93,6 +96,8 @@ def tile_localtemporalattention_pa_k_kernel(tc, attn, v, W_out, grad_out, out):
                 raw = new_chunk(position, "p (r c k)")
                 dst = raw[:].rearrange("p (r k) -> p r k", r=ROW_TILES)
                 load_features(operand, chunk * K_CHUNK, (chunk + 1) * K_CHUNK, dst)
+                if (operand, chunk) == ATTN_BEHIND:
+                    nc.sync.dma_start(out=attn_bf16[:], in_=attn.rearrange("b h s t u -> t (b h s) u"))
 
         def transpose_panel(operand, k_pass):
             chunk, pass_in_chunk = divmod(k_pass, PASSES_PER_CHUNK)
@@ -161,14 +166,19 @@ def tile_localtemporalattention_pa_k_kernel(tc, attn, v, W_out, grad_out, out):
             engine_copies = [(nc.scalar.copy, nc.scalar.copy), (nc.scalar.copy, nc.vector.tensor_copy)]
             for (operand, k_pass), panel_banks, copies in zip(fresh, banks, engine_copies):
                 regroup_panel(operand, k_pass, panel_banks, copies)
-                if operand == LAST_HALF:
-                    matrices = slice(2 * k_pass, 2 * k_pass + 2)
+                cast_turn = k_pass - (N_PASSES - CAST_PANELS)
+                if operand == LAST_HALF and cast_turn >= 0:
+                    share = N_MATRICES // CAST_PANELS
+                    matrices = slice(cast_turn * share, (cast_turn + 1) * share)
                     nc.scalar.copy(out=attn_f32[:, matrices, :], in_=attn_bf16[:, matrices, :])
             for operand, k_pass in ready:
                 if operand != GRAD:
                     multiply_pass(operand - 1, k_pass)
                     if k_pass == N_PASSES - 1:
                         save_gctx(operand - 1)
+
+        attn_bf16 = const.tile([P, N_MATRICES, T], BF16)
+        attn_f32 = const.tile([P, N_MATRICES, T], F32)
 
         new_chunk(0, "p (c r k)")
         new_chunk(1, "p (c r k)")
@@ -177,9 +187,6 @@ def tile_localtemporalattention_pa_k_kernel(tc, attn, v, W_out, grad_out, out):
                 load_features(operand, k_pass * K_PASS, (k_pass + 1) * K_PASS, panel_of[(operand, k_pass)])
         for position in range(2, RAW_BUFS):
             load_chunk(position)
-        attn_bf16 = const.tile([P, B * H * S, T], BF16)
-        attn_f32 = const.tile([P, B * H * S, T], F32)
-        nc.sync.dma_start(out=attn_bf16[:], in_=attn.rearrange("b h s t u -> t (b h s) u"))
 
         steps = [[(GRAD, k_pass), (1, k_pass)] for k_pass in range(N_PASSES)]
         steps.extend([[(LAST_HALF, k_pass), (LAST_HALF, k_pass + 1)] for k_pass in range(0, N_PASSES, 2)])

@@ -32,7 +32,6 @@ GRAD = 0
 LAST_HALF = HALVES
 ATTN_BEHIND = (LAST_HALF, 1)
 N_MATRICES = B * H * S
-CAST_PANELS = N_PASSES // 2
 
 FLOPS = 2 * B * T * S * C * CO + 2 * B * H * S * T * T * HD
 BYTES = 2 * (B * H * S * T * T + C * CO + B * T * S * CO) + 4 * B * T * S * C
@@ -155,30 +154,27 @@ def tile_localtemporalattention_pa_k_kernel(tc, attn, v, W_out, grad_out, out):
 
         def save_gctx(half):
             for i in range(ROW_TILES):
-                gctx = gctx_pool.tile([P, PANEL_ROWS], F32, name="gctx%d_%d" % (half, i))
-                alternate_copy(i)(out=gctx[:], in_=acc_of[(half, i)][:])
-                gctx_of[(half, i)] = gctx
+                hi = gctx_pool.tile([P, PANEL_ROWS], BF16, name="gctx_hi%d_%d" % (half, i))
+                lo = gctx_pool.tile([P, PANEL_ROWS], BF16, name="gctx_lo%d_%d" % (half, i))
+                nc.scalar.copy(out=hi[:], in_=acc_of[(half, i)][:])
+                nc.vector.tensor_tensor(out=lo[:], in0=acc_of[(half, i)][:], in1=hi[:], op=mybir.AluOpType.subtract)
+                gctx_of[(half, i)] = (hi, lo)
 
-        def pipeline_step(fresh, ready):
+        def pipeline_step(fresh, ready, done):
             banks = [transpose_panel(operand, k_pass) for operand, k_pass in fresh]
             for operand, k_pass in ready:
                 quantise_panel(operand, k_pass)
+            for operand, k_pass in done:
+                if operand != GRAD and k_pass == N_PASSES - 1:
+                    save_gctx(operand - 1)
             engine_copies = [(nc.scalar.copy, nc.scalar.copy), (nc.scalar.copy, nc.vector.tensor_copy)]
             for (operand, k_pass), panel_banks, copies in zip(fresh, banks, engine_copies):
                 regroup_panel(operand, k_pass, panel_banks, copies)
-                cast_turn = k_pass - (N_PASSES - CAST_PANELS)
-                if operand == LAST_HALF and cast_turn >= 0:
-                    share = N_MATRICES // CAST_PANELS
-                    matrices = slice(cast_turn * share, (cast_turn + 1) * share)
-                    nc.scalar.copy(out=attn_f32[:, matrices, :], in_=attn_bf16[:, matrices, :])
             for operand, k_pass in ready:
                 if operand != GRAD:
                     multiply_pass(operand - 1, k_pass)
-                    if k_pass == N_PASSES - 1:
-                        save_gctx(operand - 1)
 
         attn_bf16 = const.tile([P, N_MATRICES, T], BF16)
-        attn_f32 = const.tile([P, N_MATRICES, T], F32)
 
         new_chunk(0, "p (c r k)")
         new_chunk(1, "p (c r k)")
@@ -190,8 +186,8 @@ def tile_localtemporalattention_pa_k_kernel(tc, attn, v, W_out, grad_out, out):
 
         steps = [[(GRAD, k_pass), (1, k_pass)] for k_pass in range(N_PASSES)]
         steps.extend([[(LAST_HALF, k_pass), (LAST_HALF, k_pass + 1)] for k_pass in range(0, N_PASSES, 2)])
-        for fresh, ready in zip(steps + [[]], [[]] + steps):
-            pipeline_step(fresh, ready)
+        for fresh, ready, done in zip(steps + [[], []], [[]] + steps + [[]], [[], []] + steps):
+            pipeline_step(fresh, ready, done)
 
         for half in range(HALVES):
             for i in range(ROW_TILES):
@@ -199,13 +195,14 @@ def tile_localtemporalattention_pa_k_kernel(tc, attn, v, W_out, grad_out, out):
                 mixed = work_psum.tile([P, HEADS_PER_HALF, HD], F32, tag="bank", name="mixed")
                 for r in range(HEADS_PER_HALF):
                     h = half * HEADS_PER_HALF + r
-                    nc.tensor.matmul(
-                        out=mixed[:, r, :],
-                        lhsT=attn_f32[:, (b * H + h) * S + s, :],
-                        rhs=gctx_of[(half, i)][:, r * HD : (r + 1) * HD],
-                        start=True,
-                        stop=True,
-                    )
+                    for term in range(2):
+                        nc.tensor.matmul(
+                            out=mixed[:, r, :],
+                            lhsT=attn_bf16[:, (b * H + h) * S + s, :],
+                            rhs=gctx_of[(half, i)][term][:, r * HD : (r + 1) * HD],
+                            start=(term == 0),
+                            stop=(term == 1),
+                        )
                 result = result_pool.tile([P, HEADS_PER_HALF, HD], F32, tag="result", name="result")
                 alternate_copy(i)(out=result[:], in_=mixed[:])
                 first_head = half * HEADS_PER_HALF

@@ -67,6 +67,7 @@ def tile_localtemporalattention_pa_k_kernel(tc, attn, v, W_out, grad_out, out):
         codes_of = {}
         scales_of = {}
         acc_of = {}
+        whole_of = {}
         gctx_of = {}
 
         ident = const.tile([P, P], F32)
@@ -134,45 +135,69 @@ def tile_localtemporalattention_pa_k_kernel(tc, attn, v, W_out, grad_out, out):
             codes_of[(operand, k_pass)] = codes
             scales_of[(operand, k_pass)] = scales
 
-        def multiply_pass(half, k_pass):
+        def multiply_pass(half, k_pass, i):
+            if k_pass == 0:
+                acc_of[(half, i)] = acc_psum.tile([P, PANEL_ROWS], F32, tag="acc%d" % i, name="acc%d" % i)
+            rows = slice(i * P, (i + 1) * P)
+            nc.tensor.matmul_mx(
+                out=acc_of[(half, i)][:],
+                lhsT=codes_of[(GRAD, k_pass)][:, rows].bitcast(E5M2_X4),
+                lhsT_scale=scales_of[(GRAD, k_pass)][:, rows],
+                rhs=codes_of[(1 + half, k_pass)][:].bitcast(E4M3_X4),
+                rhs_scale=scales_of[(1 + half, k_pass)][:],
+                start=(k_pass == 0),
+                stop=(k_pass == N_PASSES - 1),
+            )
+
+        def park_gctx(half):
             for i in range(ROW_TILES):
-                if k_pass == 0:
-                    acc_of[(half, i)] = acc_psum.tile([P, PANEL_ROWS], F32, tag="acc%d" % i, name="acc%d" % i)
-                rows = slice(i * P, (i + 1) * P)
-                nc.tensor.matmul_mx(
-                    out=acc_of[(half, i)][:],
-                    lhsT=codes_of[(GRAD, k_pass)][:, rows].bitcast(E5M2_X4),
-                    lhsT_scale=scales_of[(GRAD, k_pass)][:, rows],
-                    rhs=codes_of[(1 + half, k_pass)][:].bitcast(E4M3_X4),
-                    rhs_scale=scales_of[(1 + half, k_pass)][:],
-                    start=(k_pass == 0),
-                    stop=(k_pass == N_PASSES - 1),
-                )
+                parked = gctx_pool.tile([P, PANEL_ROWS], F32, name="gctx_f32_%d" % i)
+                engine_copy = nc.vector.tensor_copy if i == 0 else nc.scalar.copy
+                engine_copy(out=parked[:], in_=acc_of[(half, i)][:])
+                whole_of[(half, i)] = parked
 
-        def alternate_copy(i):
-            return nc.scalar.copy if i % 2 == 0 else nc.vector.tensor_copy
+        def split_gctx(half, i):
+            whole = whole_of.get((half, i), acc_of[(half, i)])
+            hi = gctx_pool.tile([P, PANEL_ROWS], BF16, name="gctx_hi%d_%d" % (half, i))
+            lo = gctx_pool.tile([P, PANEL_ROWS], BF16, name="gctx_lo%d_%d" % (half, i))
+            nc.scalar.copy(out=hi[:], in_=whole[:])
+            nc.vector.tensor_tensor(out=lo[:], in0=whole[:], in1=hi[:], op=mybir.AluOpType.subtract)
+            gctx_of[(half, i)] = (hi, lo)
 
-        def save_gctx(half):
-            for i in range(ROW_TILES):
-                hi = gctx_pool.tile([P, PANEL_ROWS], BF16, name="gctx_hi%d_%d" % (half, i))
-                lo = gctx_pool.tile([P, PANEL_ROWS], BF16, name="gctx_lo%d_%d" % (half, i))
-                nc.scalar.copy(out=hi[:], in_=acc_of[(half, i)][:])
-                nc.vector.tensor_tensor(out=lo[:], in0=acc_of[(half, i)][:], in1=hi[:], op=mybir.AluOpType.subtract)
-                gctx_of[(half, i)] = (hi, lo)
+        def mix_frames(half, i, engine_copy):
+            b, s = divmod(i, S)
+            mixed = work_psum.tile([P, HEADS_PER_HALF, HD], F32, tag="bank", name="mixed")
+            for r in range(HEADS_PER_HALF):
+                h = half * HEADS_PER_HALF + r
+                for term in range(2):
+                    nc.tensor.matmul(
+                        out=mixed[:, r, :],
+                        lhsT=attn_bf16[:, (b * H + h) * S + s, :],
+                        rhs=gctx_of[(half, i)][term][:, r * HD : (r + 1) * HD],
+                        start=(term == 0),
+                        stop=(term == 1),
+                    )
+            result = result_pool.tile([P, HEADS_PER_HALF, HD], F32, tag="result", name="result")
+            engine_copy(out=result[:], in_=mixed[:])
+            first_head = half * HEADS_PER_HALF
+            nc.sync.dma_start(out=out[b, :, s, first_head : first_head + HEADS_PER_HALF, :], in_=result[:])
 
-        def pipeline_step(fresh, ready, done):
+        def pipeline_step(fresh, ready):
             banks = [transpose_panel(operand, k_pass) for operand, k_pass in fresh]
             for operand, k_pass in ready:
                 quantise_panel(operand, k_pass)
-            for operand, k_pass in done:
-                if operand != GRAD and k_pass == N_PASSES - 1:
-                    save_gctx(operand - 1)
             engine_copies = [(nc.scalar.copy, nc.scalar.copy), (nc.scalar.copy, nc.vector.tensor_copy)]
             for (operand, k_pass), panel_banks, copies in zip(fresh, banks, engine_copies):
                 regroup_panel(operand, k_pass, panel_banks, copies)
-            for operand, k_pass in ready:
-                if operand != GRAD:
-                    multiply_pass(operand - 1, k_pass)
+            w_ready = [(operand - 1, k_pass) for operand, k_pass in ready if operand != GRAD]
+            if fresh:
+                for half, k_pass in w_ready:
+                    for i in range(ROW_TILES):
+                        multiply_pass(half, k_pass, i)
+            else:
+                for i in range(ROW_TILES):
+                    for half, k_pass in w_ready:
+                        multiply_pass(half, k_pass, i)
 
         attn_bf16 = const.tile([P, N_MATRICES, T], BF16)
 
@@ -186,24 +211,24 @@ def tile_localtemporalattention_pa_k_kernel(tc, attn, v, W_out, grad_out, out):
 
         steps = [[(GRAD, k_pass), (1, k_pass)] for k_pass in range(N_PASSES)]
         steps.extend([[(LAST_HALF, k_pass), (LAST_HALF, k_pass + 1)] for k_pass in range(0, N_PASSES, 2)])
-        for fresh, ready, done in zip(steps + [[], []], [[]] + steps + [[]], [[], []] + steps):
-            pipeline_step(fresh, ready, done)
+        first_half_work = [
+            [],
+            [(split_gctx, (0, 0)), (split_gctx, (0, 1))],
+            [(split_gctx, (0, 2)), (split_gctx, (0, 3)), (mix_frames, (0, 0, nc.scalar.copy))],
+            [(mix_frames, (0, 1, nc.scalar.copy))],
+            [(mix_frames, (0, 2, nc.scalar.copy))],
+            [(mix_frames, (0, 3, nc.scalar.copy))],
+        ]
+        round_1_steps = N_PASSES + 1
+        for n, (fresh, ready) in enumerate(zip(steps + [[]], [[]] + steps)):
+            pipeline_step(fresh, ready)
+            if n + 1 == round_1_steps:
+                park_gctx(0)
+            elif round_1_steps <= n < round_1_steps + len(first_half_work):
+                for call, arguments in first_half_work[n - round_1_steps]:
+                    call(*arguments)
 
-        for half in range(HALVES):
-            for i in range(ROW_TILES):
-                b, s = divmod(i, S)
-                mixed = work_psum.tile([P, HEADS_PER_HALF, HD], F32, tag="bank", name="mixed")
-                for r in range(HEADS_PER_HALF):
-                    h = half * HEADS_PER_HALF + r
-                    for term in range(2):
-                        nc.tensor.matmul(
-                            out=mixed[:, r, :],
-                            lhsT=attn_bf16[:, (b * H + h) * S + s, :],
-                            rhs=gctx_of[(half, i)][term][:, r * HD : (r + 1) * HD],
-                            start=(term == 0),
-                            stop=(term == 1),
-                        )
-                result = result_pool.tile([P, HEADS_PER_HALF, HD], F32, tag="result", name="result")
-                alternate_copy(i)(out=result[:], in_=mixed[:])
-                first_head = half * HEADS_PER_HALF
-                nc.sync.dma_start(out=out[b, :, s, first_head : first_head + HEADS_PER_HALF, :], in_=result[:])
+        for i in range(ROW_TILES):
+            split_gctx(1, i)
+        for i, engine_copy in enumerate([nc.scalar.copy, nc.scalar.copy, nc.vector.tensor_copy, nc.scalar.copy]):
+            mix_frames(1, i, engine_copy)

from contextlib import ExitStack

import concourse.mybir as mybir
from concourse.masks import make_identity

F32 = mybir.dt.float32
BF16 = mybir.dt.bfloat16
U32 = mybir.dt.uint32
U8 = mybir.dt.uint8
E5M2_X4 = mybir.dt.float8_e5m2_x4
E4M3_X4 = mybir.dt.float8_e4m3fn_x4

B, T, S, H, HD = 2, 128, 2, 8, 128
C = H * HD
CO = 8192

P = 128
PACK = 4
K_PASS = P * PACK
N_PASSES = CO // K_PASS
ROW_TILES = 4
PANEL_ROWS = ROW_TILES * P
HALVES = C // PANEL_ROWS
HEADS_PER_HALF = H // HALVES

K_CHUNK = 1024
PASSES_PER_CHUNK = K_CHUNK // K_PASS
N_CHUNKS = CO // K_CHUNK
RAW_BUFS = 12

GRAD = 0
LAST_HALF = HALVES
ATTN_BEHIND = (LAST_HALF, 1)
N_MATRICES = B * H * S

FLOPS = 2 * B * T * S * C * CO + 2 * B * H * S * T * T * HD
BYTES = 2 * (B * H * S * T * T + C * CO + B * T * S * CO) + 4 * B * T * S * C


def tile_localtemporalattention_pa_k_kernel(tc, attn, v, W_out, grad_out, out):
    nc = tc.nc

    grad_rows = grad_out.rearrange("b (t s) k -> b t s k", s=S)
    w_rows = W_out.rearrange("(half r p) k -> half p r k", half=HALVES, r=ROW_TILES)

    chunk_order = []
    for chunk in range(N_CHUNKS):
        chunk_order.extend([(GRAD, chunk), (1, chunk)])
    for chunk in range(N_CHUNKS):
        chunk_order.append((LAST_HALF, chunk))

    with ExitStack() as stack:
        const = stack.enter_context(tc.tile_pool(name="const", bufs=1))
        raw_pool = stack.enter_context(tc.tile_pool(name="raw", bufs=RAW_BUFS))
        grouped_pool = stack.enter_context(tc.tile_pool(name="grouped", bufs=4))
        grad_mx = stack.enter_context(tc.tile_pool(name="grad_mx", bufs=1))
        w_mx = stack.enter_context(tc.tile_pool(name="w_mx", bufs=4))
        gctx_pool = stack.enter_context(tc.tile_pool(name="gctx", bufs=1))
        result_pool = stack.enter_context(tc.tile_pool(name="result", bufs=4))
        acc_psum = stack.enter_context(tc.psum_pool(name="acc", bufs=1))
        work_psum = stack.enter_context(tc.psum_pool(name="work", bufs=4))
        stack.enter_context(tc.manual_schedule())

        panel_of = {}
        words_of = {}
        grouped_of = {}
        codes_of = {}
        scales_of = {}
        acc_of = {}
        whole_of = {}
        gctx_of = {}

        ident = const.tile([P, P], F32)
        make_identity(nc, ident[:])

        def load_features(operand, k_lo, k_hi, dst):
            if operand == GRAD:
                for b in range(B):
                    nc.sync.dma_start(out=dst[:, S * b : S * b + S, :], in_=grad_rows[b, :, :, k_lo:k_hi])
            else:
                nc.sync.dma_start(out=dst, in_=w_rows[operand - 1, :, :, k_lo:k_hi])

        def new_chunk(position, layout):
            operand, chunk = chunk_order[position]
            raw = raw_pool.tile([P, ROW_TILES * K_CHUNK], BF16, tag="raw", name="raw")
            panels = raw[:].rearrange(layout + " -> p c r k", c=PASSES_PER_CHUNK, r=ROW_TILES)
            words = raw[:].bitcast(F32).rearrange(layout + " -> p c r k", c=PASSES_PER_CHUNK, r=ROW_TILES)
            for c in range(PASSES_PER_CHUNK):
                panel_of[(operand, chunk * PASSES_PER_CHUNK + c)] = panels[:, c]
                words_of[(operand, chunk * PASSES_PER_CHUNK + c)] = words[:, c]
            return raw

        def load_chunk(position):
            if position < len(chunk_order):
                operand, chunk = chunk_order[position]
                raw = new_chunk(position, "p (r c k)")
                dst = raw[:].rearrange("p (r k) -> p r k", r=ROW_TILES)
                load_features(operand, chunk * K_CHUNK, (chunk + 1) * K_CHUNK, dst)
                if (operand, chunk) == ATTN_BEHIND:
                    nc.sync.dma_start(out=attn_bf16[:], in_=attn.rearrange("b h s t u -> t (b h s) u"))

        def transpose_panel(operand, k_pass):
            chunk, pass_in_chunk = divmod(k_pass, PASSES_PER_CHUNK)
            words = words_of[(operand, k_pass)]
            banks = []
            for pair in range(ROW_TILES // 2):
                bank = work_psum.tile([P, 2, 2 * P], F32, tag="bank", name="bank")
                for r in range(2):
                    for u in range(2):
                        nc.tensor.transpose(
                            bank[:, u, r * P : (r + 1) * P], words[:, 2 * pair + r, u * P : (u + 1) * P], ident[:]
                        )
                banks.append(bank)
            if pass_in_chunk == PASSES_PER_CHUNK - 1:
                load_chunk(chunk_order.index((operand, chunk)) + RAW_BUFS)
            return banks

        def regroup_panel(operand, k_pass, banks, copies):
            grouped = grouped_pool.tile([P, PANEL_ROWS * PACK], BF16, tag="grouped", name="grouped", align_bytes=64)
            halves = grouped[:].bitcast(F32).rearrange("p (pair n u) -> p pair n u", pair=2, u=2)
            for pair in range(2):
                copies[pair](out=halves[:, pair], in_=banks[pair][:].rearrange("p u n -> p n u"))
            grouped_of[(operand, k_pass)] = grouped

        def quantise_panel(operand, k_pass):
            if operand == GRAD:
                codes = grad_mx.tile([P, PANEL_ROWS], U32, name="grad_codes%d" % k_pass, align_bytes=64)
                scales = grad_mx.tile([P, PANEL_ROWS], U8, name="grad_scales%d" % k_pass, align_bytes=64)
                fp8_x4 = E5M2_X4
            else:
                codes = w_mx.tile([P, PANEL_ROWS], U32, tag="w_codes", name="w_codes", align_bytes=64)
                scales = w_mx.tile([P, PANEL_ROWS], U8, tag="w_scales", name="w_scales", align_bytes=64)
                fp8_x4 = E4M3_X4
            nc.vector.quantize_mx(out=codes[:].bitcast(fp8_x4), scales=scales[:], in_=grouped_of[(operand, k_pass)][:])
            codes_of[(operand, k_pass)] = codes
            scales_of[(operand, k_pass)] = scales

        def multiply_pass(half, k_pass, i):
            if k_pass == 0:
                acc_of[(half, i)] = acc_psum.tile([P, PANEL_ROWS], F32, tag="acc%d" % i, name="acc%d" % i)
            rows = slice(i * P, (i + 1) * P)
            nc.tensor.matmul_mx(
                out=acc_of[(half, i)][:],
                lhsT=codes_of[(GRAD, k_pass)][:, rows].bitcast(E5M2_X4),
                lhsT_scale=scales_of[(GRAD, k_pass)][:, rows],
                rhs=codes_of[(1 + half, k_pass)][:].bitcast(E4M3_X4),
                rhs_scale=scales_of[(1 + half, k_pass)][:],
                start=(k_pass == 0),
                stop=(k_pass == N_PASSES - 1),
            )

        def park_gctx(half):
            for i in range(ROW_TILES):
                parked = gctx_pool.tile([P, PANEL_ROWS], F32, name="gctx_f32_%d" % i)
                engine_copy = nc.vector.tensor_copy if i == 0 else nc.scalar.copy
                engine_copy(out=parked[:], in_=acc_of[(half, i)][:])
                whole_of[(half, i)] = parked

        def split_gctx(half, i):
            whole = whole_of.get((half, i), acc_of[(half, i)])
            hi = gctx_pool.tile([P, PANEL_ROWS], BF16, name="gctx_hi%d_%d" % (half, i))
            lo = gctx_pool.tile([P, PANEL_ROWS], BF16, name="gctx_lo%d_%d" % (half, i))
            nc.scalar.copy(out=hi[:], in_=whole[:])
            nc.vector.tensor_tensor(out=lo[:], in0=whole[:], in1=hi[:], op=mybir.AluOpType.subtract)
            gctx_of[(half, i)] = (hi, lo)

        def mix_frames(half, i, engine_copy):
            b, s = divmod(i, S)
            mixed = work_psum.tile([P, HEADS_PER_HALF, HD], F32, tag="bank", name="mixed")
            for r in range(HEADS_PER_HALF):
                h = half * HEADS_PER_HALF + r
                for term in range(2):
                    nc.tensor.matmul(
                        out=mixed[:, r, :],
                        lhsT=attn_bf16[:, (b * H + h) * S + s, :],
                        rhs=gctx_of[(half, i)][term][:, r * HD : (r + 1) * HD],
                        start=(term == 0),
                        stop=(term == 1),
                    )
            result = result_pool.tile([P, HEADS_PER_HALF, HD], F32, tag="result", name="result")
            engine_copy(out=result[:], in_=mixed[:])
            first_head = half * HEADS_PER_HALF
            nc.sync.dma_start(out=out[b, :, s, first_head : first_head + HEADS_PER_HALF, :], in_=result[:])

        def pipeline_step(fresh, ready):
            banks = [transpose_panel(operand, k_pass) for operand, k_pass in fresh]
            for operand, k_pass in ready:
                quantise_panel(operand, k_pass)
            engine_copies = [(nc.scalar.copy, nc.scalar.copy), (nc.scalar.copy, nc.vector.tensor_copy)]
            for (operand, k_pass), panel_banks, copies in zip(fresh, banks, engine_copies):
                regroup_panel(operand, k_pass, panel_banks, copies)
            w_ready = [(operand - 1, k_pass) for operand, k_pass in ready if operand != GRAD]
            if fresh:
                for half, k_pass in w_ready:
                    for i in range(ROW_TILES):
                        multiply_pass(half, k_pass, i)
            else:
                for i in range(ROW_TILES):
                    for half, k_pass in w_ready:
                        multiply_pass(half, k_pass, i)

        attn_bf16 = const.tile([P, N_MATRICES, T], BF16)

        new_chunk(0, "p (c r k)")
        new_chunk(1, "p (c r k)")
        for k_pass in range(PASSES_PER_CHUNK):
            for operand in (GRAD, 1):
                load_features(operand, k_pass * K_PASS, (k_pass + 1) * K_PASS, panel_of[(operand, k_pass)])
        for position in range(2, RAW_BUFS):
            load_chunk(position)

        steps = [[(GRAD, k_pass), (1, k_pass)] for k_pass in range(N_PASSES)]
        steps.extend([[(LAST_HALF, k_pass), (LAST_HALF, k_pass + 1)] for k_pass in range(0, N_PASSES, 2)])
        first_half_work = [
            [],
            [(split_gctx, (0, 0)), (split_gctx, (0, 1))],
            [(split_gctx, (0, 2)), (split_gctx, (0, 3)), (mix_frames, (0, 0, nc.scalar.copy))],
            [(mix_frames, (0, 1, nc.scalar.copy))],
            [(mix_frames, (0, 2, nc.scalar.copy))],
            [(mix_frames, (0, 3, nc.scalar.copy))],
        ]
        round_1_steps = N_PASSES + 1
        for n, (fresh, ready) in enumerate(zip(steps + [[]], [[]] + steps)):
            pipeline_step(fresh, ready)
            if n + 1 == round_1_steps:
                park_gctx(0)
            elif round_1_steps <= n < round_1_steps + len(first_half_work):
                for call, arguments in first_half_work[n - round_1_steps]:
                    call(*arguments)

        for i in range(ROW_TILES):
            split_gctx(1, i)
        for i, engine_copy in enumerate([nc.scalar.copy, nc.scalar.copy, nc.vector.tensor_copy, nc.scalar.copy]):
            mix_frames(1, i, engine_copy)
